import numpy as np
import ml_dtypes


def mxq(x, axis, fmt="e4m3"):
    dtype, down = {"e4m3": (ml_dtypes.float8_e4m3fn, 7), "e5m2": (ml_dtypes.float8_e5m2, 14)}[fmt]
    v = np.moveaxis(np.asarray(x, np.float32).astype(ml_dtypes.bfloat16).astype(np.float64), axis, -1)
    blocks = v.reshape(v.shape[:-1] + (-1, 32))
    amax = np.abs(blocks).max(-1, keepdims=True)
    byte = np.maximum(np.where(amax > 0, np.frexp(amax)[1] - 1 + 127, 0) - down, 1)
    scale = np.exp2(byte - 127.0)
    codes = (blocks / scale).astype(np.float32).astype(dtype).astype(np.float64)
    return np.moveaxis((codes * scale).reshape(v.shape), -1, axis)


WIDE = False


def mx_kscale(k):
    if not WIDE:
        return np.ones(k)
    levels = np.array([10, -10, 5, -5, 0])
    a = np.random.permutation(np.resize(levels, k // 512 * 4)).reshape(k // 512, 4)
    idx = np.arange(k)
    return np.exp2(a[idx // 512, idx % 128 // 32])


BF16 = ml_dtypes.bfloat16


def bf(x):
    return np.asarray(x, np.float32).astype(BF16)


def f64(x):
    return np.asarray(x).astype(np.float64)


N_A, N_P, D = 512, 512, 8192
TEMPERATURE = 0.07
SIG = 3.5
SA = np.sqrt(SIG * TEMPERATURE / np.sqrt(D))
SP = SA * np.sqrt(SIG ** 2 - 2.0 * np.log(N_P / N_A)) / SIG


def logsumexp(v):
    m = v.max(axis=1, keepdims=True)
    return m[:, 0] + np.log(np.exp(v - m).sum(axis=1))


def setup_inputs():
    s = mx_kscale(D)
    c = np.mean(s ** 4) ** -0.25
    return {"anchor": bf(np.random.standard_normal((N_A, D)) * SA * s * c),
            "pos": bf(np.random.standard_normal((N_P, D)) * SP / (s * c))}


def reference(anchor, pos):
    aq = mxq(f64(anchor), 1, "e4m3")
    sim_pos = (aq @ mxq(f64(pos), 1, "e4m3").T) / TEMPERATURE
    sim_neg = (aq @ aq.T) / TEMPERATURE
    sim_neg = np.where(np.eye(aq.shape[0], dtype=bool), -np.inf, sim_neg)
    numerator = logsumexp(sim_pos)
    denominator = np.logaddexp(numerator, logsumexp(sim_neg))
    return numerator - denominator

@@ -1,0 +1,181 @@
+from contextlib import ExitStack
+
+import concourse.masks as masks
+import concourse.mybir as mybir
+
+F32 = mybir.dt.float32
+BF16 = mybir.dt.bfloat16
+U32 = mybir.dt.uint32
+U8 = mybir.dt.uint8
+FP8X4 = mybir.dt.float8_e4m3fn_x4
+ACT = mybir.ActivationFunctionType
+ALU = mybir.AluOpType
+AXIS = mybir.AxisListType
+
+P = 128
+PACK = 4
+K_PASS = P * PACK
+ROWS = 512
+ROW_TILES = ROWS // P
+FEATURES = 8192
+PASSES = FEATURES // K_PASS
+RUN_PASSES = 2
+RUN_FEATURES = RUN_PASSES * K_PASS
+RUNS = PASSES // RUN_PASSES
+ALL_RUNS = 2 * RUNS
+LOADS_AHEAD = 6
+BANK_TILES = 2
+TEMPERATURE = 0.07
+MASKED = -1.0e30
+POS, NEG = 0, 1
+
+FLOPS = 2 * 2 * ROWS * ROWS * FEATURES
+
+
+def tile_crossgenderinfonceloss_pa_k_kernel(tc, anchor, pos, out):
+    nc = tc.nc
+    with ExitStack() as ctx:
+        const = ctx.enter_context(tc.tile_pool(name="const", bufs=1))
+        keep = ctx.enter_context(tc.tile_pool(name="keep", bufs=1))
+        raw_pool = ctx.enter_context(tc.tile_pool(name="raw", bufs=LOADS_AHEAD + 1))
+        grouped_pool = ctx.enter_context(tc.tile_pool(name="grouped", bufs=3))
+        sum_banks = ctx.enter_context(tc.psum_pool(name="sum_banks", bufs=1))
+        turn_banks = ctx.enter_context(tc.psum_pool(name="turn_banks", bufs=4))
+        ctx.enter_context(tc.manual_schedule())
+
+        sources = [x.rearrange("(i p) k -> p i k", p=P) for x in (anchor, pos)]
+
+        codes = keep.tile([P, 2 * PASSES * ROWS], U32, align_bytes=64)
+        scales = keep.tile([P, 2 * PASSES * ROWS], U8, align_bytes=64)
+
+        neg_logits = keep.tile([P, ROW_TILES, ROWS], F32)
+        spent = keep.tile([P, 2, ROW_TILES, ROWS], F32)
+        maxima = keep.tile([P, 2, ROW_TILES], F32)
+        shifts = keep.tile([P, 2, ROW_TILES], F32)
+        sums = keep.tile([P, 2, ROW_TILES], F32)
+
+        def load_run(s):
+            raw = raw_pool.tile([P, ROW_TILES, RUN_FEATURES], BF16)
+            first = (s % RUNS) * RUN_FEATURES
+            nc.sync.dma_start(out=raw[:], in_=sources[s // RUNS][:, :, first : first + RUN_FEATURES])
+            return raw
+
+        def transpose_run(raw):
+            grouped = grouped_pool.tile([P, RUN_PASSES, ROWS, PACK], BF16, align_bytes=64)
+            raw_words = raw[:].bitcast(F32)
+            grouped_words = grouped[:].bitcast(F32)
+            for g in range(RUN_PASSES):
+                for b in range(ROW_TILES // BANK_TILES):
+                    bank = turn_banks.tile([P, 2, BANK_TILES * P], F32)
+                    for j in range(BANK_TILES):
+                        for u in range(2):
+                            first = (2 * g + u) * P
+                            nc.tensor.transpose(
+                                bank[:, u, j * P : (j + 1) * P],
+                                raw_words[:, b * BANK_TILES + j, first : first + P],
+                                identity[:],
+                            )
+                    copy_out = nc.scalar.copy if b % 2 == 0 else nc.vector.tensor_copy
+                    columns = slice(b * BANK_TILES * P, (b + 1) * BANK_TILES * P)
+                    copy_out(out=grouped_words[:, g, columns, :], in_=bank[:].rearrange("q u r -> q r u"))
+            return grouped
+
+        def quantise_run(s, grouped):
+            columns = slice(s * RUN_PASSES * ROWS, (s + 1) * RUN_PASSES * ROWS)
+            nc.vector.quantize_mx(
+                out=codes[:, columns].bitcast(FP8X4),
+                scales=scales[:, columns],
+                in_=grouped[:].rearrange("q g r t -> q (g r t)"),
+            )
+
+        def new_sums():
+            return [sum_banks.tile([P, ROWS], F32, name="sum%d" % i, tag="sum%d" % i) for i in range(ROW_TILES)]
+
+        def multiply_run(s, banks):
+            for i in range(ROW_TILES):
+                for g in range(RUN_PASSES):
+                    c = (s % RUNS) * RUN_PASSES + g
+                    stationary = slice(c * ROWS + i * P, c * ROWS + (i + 1) * P)
+                    moving = slice((s * RUN_PASSES + g) * ROWS, (s * RUN_PASSES + g + 1) * ROWS)
+                    nc.tensor.matmul_mx(
+                        out=banks[i][:],
+                        lhsT=codes[:, stationary].bitcast(FP8X4),
+                        lhsT_scale=scales[:, stationary],
+                        rhs=codes[:, moving].bitcast(FP8X4),
+                        rhs_scale=scales[:, moving],
+                        start=(c == 0),
+                        stop=(c == PASSES - 1),
+                    )
+
+        def sum_exponentials(which, i, logits):
+            one = slice(i, i + 1)
+            nc.vector.reduce_max(out=maxima[:, which, one], in_=logits, axis=AXIS.X)
+            nc.vector.tensor_scalar_mul(out=shifts[:, which, one], in0=maxima[:, which, one], scalar1=-1.0 / TEMPERATURE)
+            nc.scalar.activation(
+                out=spent[:, which, i, :],
+                in_=logits,
+                func=ACT.Exp,
+                bias=shifts[:, which, one],
+                scale=1.0 / TEMPERATURE,
+                accum_out=sums[:, which, one],
+            )
+
+        raws = {}
+        for s in range(LOADS_AHEAD):
+            raws[s] = load_run(s)
+
+        identity = const.tile([P, P], F32)
+        masks.make_identity(nc, identity[:])
+        masked_diagonal = const.tile([P, P], F32)
+        nc.vector.tensor_scalar_mul(out=masked_diagonal[:], in0=identity[:], scalar1=MASKED)
+        result = keep.tile([P, P], F32)
+        nc.vector.memset(result[:], 0.0)
+        warm = const.tile([P, 1], F32)
+        nc.vector.memset(warm[:], 0.0)
+        nc.scalar.activation(out=warm[:], in_=warm[:], func=ACT.Exp)
+
+        banks = new_sums()
+        for s in range(ALL_RUNS):
+            if s + LOADS_AHEAD < ALL_RUNS:
+                raws[s + LOADS_AHEAD] = load_run(s + LOADS_AHEAD)
+            grouped = transpose_run(raws[s])
+            if s > 0:
+                multiply_run(s - 1, banks)
+            quantise_run(s, grouped)
+            if s == RUNS:
+                for i in range(ROW_TILES):
+                    nc.scalar.copy(out=neg_logits[:, i, :], in_=banks[i][:])
+                banks = new_sums()
+            i = s - (RUNS + 1)
+            if 0 <= i < ROW_TILES:
+                diagonal = neg_logits[:, i, i * P : (i + 1) * P]
+                nc.vector.tensor_add(out=diagonal, in0=diagonal, in1=masked_diagonal[:])
+                sum_exponentials(NEG, i, neg_logits[:, i, :])
+        multiply_run(ALL_RUNS - 1, banks)
+        for i in range(ROW_TILES):
+            sum_exponentials(POS, i, banks[i][:])
+
+        top = keep.tile([P, ROW_TILES], F32)
+        gaps = keep.tile([P, 2, ROW_TILES], F32)
+        weights = keep.tile([P, 2, ROW_TILES], F32)
+        weighted = keep.tile([P, 2, ROW_TILES], F32)
+        total = keep.tile([P, ROW_TILES], F32)
+        log_pos = keep.tile([P, ROW_TILES], F32)
+        log_total = keep.tile([P, ROW_TILES], F32)
+        numerator = keep.tile([P, ROW_TILES], F32)
+        nc.vector.tensor_max(out=top[:], in0=maxima[:, POS, :], in1=maxima[:, NEG, :])
+        nc.vector.tensor_sub(out=gaps[:], in0=maxima[:], in1=top[:].unsqueeze(1).to_broadcast([P, 2, ROW_TILES]))
+        nc.scalar.activation(out=weights[:], in_=gaps[:], func=ACT.Exp, scale=1.0 / TEMPERATURE)
+        nc.scalar.activation(out=log_pos[:], in_=sums[:, POS, :], func=ACT.Ln)
+        nc.vector.tensor_mul(out=weighted[:], in0=sums[:], in1=weights[:])
+        nc.vector.tensor_add(out=total[:], in0=weighted[:, POS, :], in1=weighted[:, NEG, :])
+        nc.scalar.activation(out=log_total[:], in_=total[:], func=ACT.Ln)
+        nc.vector.scalar_tensor_tensor(
+            out=numerator[:], in0=gaps[:, POS, :], scalar=1.0 / TEMPERATURE, in1=log_pos[:], op0=ALU.mult, op1=ALU.add
+        )
+        nc.vector.tensor_sub(out=result[:, :ROW_TILES], in0=numerator[:], in1=log_total[:])
+        turned = turn_banks.tile([P, P], F32, tag="bank")
+        nc.tensor.transpose(turned[:], result[:], identity[:])
+        result_rows = keep.tile([P, P], F32)
+        nc.vector.tensor_copy(out=result_rows[:], in_=turned[:])
+        nc.sync.dma_start(out=out.rearrange("(i p) -> i p", p=P), in_=result_rows[:ROW_TILES, :])

@@ -25,6 +25,9 @@ RUNS = PASSES // RUN_PASSES
 ALL_RUNS = 2 * RUNS
 LOADS_AHEAD = 6
 BANK_TILES = 2
+UPPER_TILES = (0, 1)
+LOWER_TILES = (2, 3)
+HALF = ROWS // 2
 TEMPERATURE = 0.07
 MASKED = -1.0e30
 POS, NEG = 0, 1
@@ -93,12 +96,13 @@ def tile_crossgenderinfonceloss_pa_k_kernel(tc, anchor, pos, out):
 
         def multiply_run(s, banks):
             for i in range(ROW_TILES):
+                left_out = HALF if s < RUNS and i in LOWER_TILES else 0
                 for g in range(RUN_PASSES):
                     c = (s % RUNS) * RUN_PASSES + g
                     stationary = slice(c * ROWS + i * P, c * ROWS + (i + 1) * P)
-                    moving = slice((s * RUN_PASSES + g) * ROWS, (s * RUN_PASSES + g + 1) * ROWS)
+                    moving = slice((s * RUN_PASSES + g) * ROWS + left_out, (s * RUN_PASSES + g + 1) * ROWS)
                     nc.tensor.matmul_mx(
-                        out=banks[i][:],
+                        out=banks[i][:, left_out:],
                         lhsT=codes[:, stationary].bitcast(FP8X4),
                         lhsT_scale=scales[:, stationary],
                         rhs=codes[:, moving].bitcast(FP8X4),
@@ -106,6 +110,16 @@ def tile_crossgenderinfonceloss_pa_k_kernel(tc, anchor, pos, out):
                         start=(c == 0),
                         stop=(c == PASSES - 1),
                     )
+
+        def sim_neg_leaves_psum(tiles, banks):
+            for i in tiles:
+                copy_out = nc.scalar.copy if i % 2 == 0 else nc.vector.tensor_copy
+                copy_out(out=neg_logits[:, i, :], in_=banks[i][:])
+
+        def mirror_sim_neg(banks):
+            for i in LOWER_TILES:
+                for j in UPPER_TILES:
+                    nc.tensor.transpose(banks[i][:, j * P : (j + 1) * P], neg_logits[:, j, i * P : (i + 1) * P], identity[:])
 
         def sum_exponentials(which, i, logits):
             one = slice(i, i + 1)
@@ -139,14 +153,16 @@ def tile_crossgenderinfonceloss_pa_k_kernel(tc, anchor, pos, out):
             if s + LOADS_AHEAD < ALL_RUNS:
                 raws[s + LOADS_AHEAD] = load_run(s + LOADS_AHEAD)
             grouped = transpose_run(raws[s])
+            if s == RUNS + 1:
+                mirror_sim_neg(banks)
+                sim_neg_leaves_psum(LOWER_TILES, banks)
+                banks = new_sums()
             if s > 0:
                 multiply_run(s - 1, banks)
             quantise_run(s, grouped)
             if s == RUNS:
-                for i in range(ROW_TILES):
-                    nc.scalar.copy(out=neg_logits[:, i, :], in_=banks[i][:])
-                banks = new_sums()
-            i = s - (RUNS + 1)
+                sim_neg_leaves_psum(UPPER_TILES, banks)
+            i = s - (RUNS + 2)
             if 0 <= i < ROW_TILES:
                 diagonal = neg_logits[:, i, i * P : (i + 1) * P]
                 nc.vector.tensor_add(out=diagonal, in0=diagonal, in1=masked_diagonal[:])

@@ -19,11 +19,12 @@ ROWS = 512
 ROW_TILES = ROWS // P
 FEATURES = 8192
 PASSES = FEATURES // K_PASS
-RUN_PASSES = 2
-RUN_FEATURES = RUN_PASSES * K_PASS
-RUNS = PASSES // RUN_PASSES
-ALL_RUNS = 2 * RUNS
+LOAD_PASSES = 2
+LOAD_FEATURES = LOAD_PASSES * K_PASS
+LOADS = PASSES // LOAD_PASSES
+ALL_LOADS = 2 * LOADS
 LOADS_AHEAD = 6
+RUN_LOADS = 2
 BANK_TILES = 2
 UPPER_TILES = (0, 1)
 LOWER_TILES = (2, 3)
@@ -57,25 +58,25 @@ def tile_crossgenderinfonceloss_pa_k_kernel(tc, anchor, pos, out):
         shifts = keep.tile([P, 2, ROW_TILES], F32)
         sums = keep.tile([P, 2, ROW_TILES], F32)
 
-        def load_run(s):
-            raw = raw_pool.tile([P, ROW_TILES, RUN_FEATURES], BF16)
-            first = (s % RUNS) * RUN_FEATURES
-            nc.sync.dma_start(out=raw[:], in_=sources[s // RUNS][:, :, first : first + RUN_FEATURES])
+        def start_load(n):
+            raw = raw_pool.tile([P, ROW_TILES, LOAD_FEATURES], BF16)
+            feature = (n % LOADS) * LOAD_FEATURES
+            nc.sync.dma_start(out=raw[:], in_=sources[n // LOADS][:, :, feature : feature + LOAD_FEATURES])
             return raw
 
-        def transpose_run(raw):
-            grouped = grouped_pool.tile([P, RUN_PASSES, ROWS, PACK], BF16, align_bytes=64)
+        def transpose_load(raw):
+            grouped = grouped_pool.tile([P, LOAD_PASSES, ROWS, PACK], BF16, align_bytes=64)
             raw_words = raw[:].bitcast(F32)
             grouped_words = grouped[:].bitcast(F32)
-            for g in range(RUN_PASSES):
+            for g in range(LOAD_PASSES):
                 for b in range(ROW_TILES // BANK_TILES):
                     bank = turn_banks.tile([P, 2, BANK_TILES * P], F32)
                     for j in range(BANK_TILES):
                         for u in range(2):
-                            first = (2 * g + u) * P
+                            word = (2 * g + u) * P
                             nc.tensor.transpose(
                                 bank[:, u, j * P : (j + 1) * P],
-                                raw_words[:, b * BANK_TILES + j, first : first + P],
+                                raw_words[:, b * BANK_TILES + j, word : word + P],
                                 identity[:],
                             )
                     copy_out = nc.scalar.copy if b % 2 == 0 else nc.vector.tensor_copy
@@ -83,8 +84,8 @@ def tile_crossgenderinfonceloss_pa_k_kernel(tc, anchor, pos, out):
                     copy_out(out=grouped_words[:, g, columns, :], in_=bank[:].rearrange("q u r -> q r u"))
             return grouped
 
-        def quantise_run(s, grouped):
-            columns = slice(s * RUN_PASSES * ROWS, (s + 1) * RUN_PASSES * ROWS)
+        def quantise_load(n, grouped):
+            columns = slice(n * LOAD_PASSES * ROWS, (n + 1) * LOAD_PASSES * ROWS)
             nc.vector.quantize_mx(
                 out=codes[:, columns].bitcast(FP8X4),
                 scales=scales[:, columns],
@@ -94,13 +95,13 @@ def tile_crossgenderinfonceloss_pa_k_kernel(tc, anchor, pos, out):
         def new_sums():
             return [sum_banks.tile([P, ROWS], F32, name="sum%d" % i, tag="sum%d" % i) for i in range(ROW_TILES)]
 
-        def multiply_run(s, banks):
+        def multiply_load(n, banks):
             for i in range(ROW_TILES):
-                left_out = HALF if s < RUNS and i in LOWER_TILES else 0
-                for g in range(RUN_PASSES):
-                    c = (s % RUNS) * RUN_PASSES + g
+                left_out = HALF if n < LOADS and i in LOWER_TILES else 0
+                for g in range(LOAD_PASSES):
+                    c = (n % LOADS) * LOAD_PASSES + g
                     stationary = slice(c * ROWS + i * P, c * ROWS + (i + 1) * P)
-                    moving = slice((s * RUN_PASSES + g) * ROWS + left_out, (s * RUN_PASSES + g + 1) * ROWS)
+                    moving = slice((n * LOAD_PASSES + g) * ROWS + left_out, (n * LOAD_PASSES + g + 1) * ROWS)
                     nc.tensor.matmul_mx(
                         out=banks[i][:, left_out:],
                         lhsT=codes[:, stationary].bitcast(FP8X4),
@@ -111,20 +112,19 @@ def tile_crossgenderinfonceloss_pa_k_kernel(tc, anchor, pos, out):
                         stop=(c == PASSES - 1),
                     )
 
-        def sim_neg_leaves_psum(tiles, banks):
-            for i in tiles:
-                copy_out = nc.scalar.copy if i % 2 == 0 else nc.vector.tensor_copy
-                copy_out(out=neg_logits[:, i, :], in_=banks[i][:])
-
-        def mirror_sim_neg(banks):
+        def sim_neg_leaves_psum(banks):
+            for j in UPPER_TILES:
+                nc.scalar.copy(out=neg_logits[:, j, :], in_=banks[j][:])
             for i in LOWER_TILES:
                 for j in UPPER_TILES:
                     nc.tensor.transpose(banks[i][:, j * P : (j + 1) * P], neg_logits[:, j, i * P : (i + 1) * P], identity[:])
+            for i in LOWER_TILES:
+                nc.scalar.copy(out=neg_logits[:, i, :], in_=banks[i][:])
 
         def sum_exponentials(which, i, logits):
             one = slice(i, i + 1)
             nc.vector.reduce_max(out=maxima[:, which, one], in_=logits, axis=AXIS.X)
-            nc.vector.tensor_scalar_mul(out=shifts[:, which, one], in0=maxima[:, which, one], scalar1=-1.0 / TEMPERATURE)
+            nc.scalar.mul(out=shifts[:, which, one], in_=maxima[:, which, one], mul=-1.0 / TEMPERATURE)
             nc.scalar.activation(
                 out=spent[:, which, i, :],
                 in_=logits,
@@ -135,8 +135,8 @@ def tile_crossgenderinfonceloss_pa_k_kernel(tc, anchor, pos, out):
             )
 
         raws = {}
-        for s in range(LOADS_AHEAD):
-            raws[s] = load_run(s)
+        for n in range(LOADS_AHEAD):
+            raws[n] = start_load(n)
 
         identity = const.tile([P, P], F32)
         masks.make_identity(nc, identity[:])
@@ -149,25 +149,22 @@ def tile_crossgenderinfonceloss_pa_k_kernel(tc, anchor, pos, out):
         nc.scalar.activation(out=warm[:], in_=warm[:], func=ACT.Exp)
 
         banks = new_sums()
-        for s in range(ALL_RUNS):
-            if s + LOADS_AHEAD < ALL_RUNS:
-                raws[s + LOADS_AHEAD] = load_run(s + LOADS_AHEAD)
-            grouped = transpose_run(raws[s])
-            if s == RUNS + 1:
-                mirror_sim_neg(banks)
-                sim_neg_leaves_psum(LOWER_TILES, banks)
-                banks = new_sums()
-            if s > 0:
-                multiply_run(s - 1, banks)
-            quantise_run(s, grouped)
-            if s == RUNS:
-                sim_neg_leaves_psum(UPPER_TILES, banks)
-            i = s - (RUNS + 2)
+        for n in range(ALL_LOADS):
+            if n + LOADS_AHEAD < ALL_LOADS:
+                raws[n + LOADS_AHEAD] = start_load(n + LOADS_AHEAD)
+            quantise_load(n, transpose_load(raws[n]))
+            if n % RUN_LOADS == RUN_LOADS - 1:
+                for m in range(max(n - RUN_LOADS, 0), n):
+                    if m == LOADS:
+                        sim_neg_leaves_psum(banks)
+                        banks = new_sums()
+                    multiply_load(m, banks)
+            i = n - (LOADS + RUN_LOADS)
             if 0 <= i < ROW_TILES:
                 diagonal = neg_logits[:, i, i * P : (i + 1) * P]
                 nc.vector.tensor_add(out=diagonal, in0=diagonal, in1=masked_diagonal[:])
                 sum_exponentials(NEG, i, neg_logits[:, i, :])
-        multiply_run(ALL_RUNS - 1, banks)
+        multiply_load(ALL_LOADS - 1, banks)
         for i in range(ROW_TILES):
             sum_exponentials(POS, i, banks[i][:])
 

@@ -10,7 +10,6 @@ U8 = mybir.dt.uint8
 FP8X4 = mybir.dt.float8_e4m3fn_x4
 ACT = mybir.ActivationFunctionType
 ALU = mybir.AluOpType
-AXIS = mybir.AxisListType
 
 P = 128
 PACK = 4
@@ -24,7 +23,6 @@ LOAD_FEATURES = LOAD_PASSES * K_PASS
 LOADS = PASSES // LOAD_PASSES
 ALL_LOADS = 2 * LOADS
 LOADS_AHEAD = 6
-RUN_LOADS = 2
 BANK_TILES = 2
 UPPER_TILES = (0, 1)
 LOWER_TILES = (2, 3)
@@ -53,8 +51,7 @@ def tile_crossgenderinfonceloss_pa_k_kernel(tc, anchor, pos, out):
         scales = keep.tile([P, 2 * PASSES * ROWS], U8, align_bytes=64)
 
         neg_logits = keep.tile([P, ROW_TILES, ROWS], F32)
-        spent = keep.tile([P, 2, ROW_TILES, ROWS], F32)
-        maxima = keep.tile([P, 2, ROW_TILES], F32)
+        negated = keep.tile([P, 2, ROW_TILES, ROWS], F32)
         shifts = keep.tile([P, 2, ROW_TILES], F32)
         sums = keep.tile([P, 2, ROW_TILES], F32)
 
@@ -112,25 +109,33 @@ def tile_crossgenderinfonceloss_pa_k_kernel(tc, anchor, pos, out):
                         stop=(c == PASSES - 1),
                     )
 
-        def sim_neg_leaves_psum(banks):
-            for j in UPPER_TILES:
-                nc.scalar.copy(out=neg_logits[:, j, :], in_=banks[j][:])
+        def sim_neg_leaves_psum(tiles, banks):
+            for i in tiles:
+                copy_out = nc.scalar.copy if i % 2 == 0 else nc.vector.tensor_copy
+                copy_out(out=neg_logits[:, i, :], in_=banks[i][:])
+
+        def mirror_sim_neg(banks):
             for i in LOWER_TILES:
                 for j in UPPER_TILES:
                     nc.tensor.transpose(banks[i][:, j * P : (j + 1) * P], neg_logits[:, j, i * P : (i + 1) * P], identity[:])
-            for i in LOWER_TILES:
-                nc.scalar.copy(out=neg_logits[:, i, :], in_=banks[i][:])
 
         def sum_exponentials(which, i, logits):
             one = slice(i, i + 1)
-            nc.vector.reduce_max(out=maxima[:, which, one], in_=logits, axis=AXIS.X)
-            nc.scalar.mul(out=shifts[:, which, one], in_=maxima[:, which, one], mul=-1.0 / TEMPERATURE)
+            nc.vector.tensor_scalar(
+                out=negated[:, which, i, :],
+                in0=logits,
+                scalar1=-1.0 / TEMPERATURE,
+                scalar2=None,
+                op0=ALU.mult,
+                op1=ALU.min,
+                accum_out=shifts[:, which, one],
+            )
             nc.scalar.activation(
-                out=spent[:, which, i, :],
-                in_=logits,
+                out=negated[:, which, i, :],
+                in_=negated[:, which, i, :],
                 func=ACT.Exp,
                 bias=shifts[:, which, one],
-                scale=1.0 / TEMPERATURE,
+                scale=-1.0,
                 accum_out=sums[:, which, one],
             )
 
@@ -152,14 +157,17 @@ def tile_crossgenderinfonceloss_pa_k_kernel(tc, anchor, pos, out):
         for n in range(ALL_LOADS):
             if n + LOADS_AHEAD < ALL_LOADS:
                 raws[n + LOADS_AHEAD] = start_load(n + LOADS_AHEAD)
-            quantise_load(n, transpose_load(raws[n]))
-            if n % RUN_LOADS == RUN_LOADS - 1:
-                for m in range(max(n - RUN_LOADS, 0), n):
-                    if m == LOADS:
-                        sim_neg_leaves_psum(banks)
-                        banks = new_sums()
-                    multiply_load(m, banks)
-            i = n - (LOADS + RUN_LOADS)
+            grouped = transpose_load(raws[n])
+            if n == LOADS + 1:
+                mirror_sim_neg(banks)
+                sim_neg_leaves_psum(LOWER_TILES, banks)
+                banks = new_sums()
+            if n > 0:
+                multiply_load(n - 1, banks)
+            quantise_load(n, grouped)
+            if n == LOADS:
+                sim_neg_leaves_psum(UPPER_TILES, banks)
+            i = n - (LOADS + 2)
             if 0 <= i < ROW_TILES:
                 diagonal = neg_logits[:, i, i * P : (i + 1) * P]
                 nc.vector.tensor_add(out=diagonal, in0=diagonal, in1=masked_diagonal[:])
@@ -168,7 +176,7 @@ def tile_crossgenderinfonceloss_pa_k_kernel(tc, anchor, pos, out):
         for i in range(ROW_TILES):
             sum_exponentials(POS, i, banks[i][:])
 
-        top = keep.tile([P, ROW_TILES], F32)
+        minus_top = keep.tile([P, ROW_TILES], F32)
         gaps = keep.tile([P, 2, ROW_TILES], F32)
         weights = keep.tile([P, 2, ROW_TILES], F32)
         weighted = keep.tile([P, 2, ROW_TILES], F32)
@@ -176,16 +184,14 @@ def tile_crossgenderinfonceloss_pa_k_kernel(tc, anchor, pos, out):
         log_pos = keep.tile([P, ROW_TILES], F32)
         log_total = keep.tile([P, ROW_TILES], F32)
         numerator = keep.tile([P, ROW_TILES], F32)
-        nc.vector.tensor_max(out=top[:], in0=maxima[:, POS, :], in1=maxima[:, NEG, :])
-        nc.vector.tensor_sub(out=gaps[:], in0=maxima[:], in1=top[:].unsqueeze(1).to_broadcast([P, 2, ROW_TILES]))
-        nc.scalar.activation(out=weights[:], in_=gaps[:], func=ACT.Exp, scale=1.0 / TEMPERATURE)
+        nc.vector.tensor_tensor(out=minus_top[:], in0=shifts[:, POS, :], in1=shifts[:, NEG, :], op=ALU.min)
+        nc.vector.tensor_sub(out=gaps[:], in0=minus_top[:].unsqueeze(1).to_broadcast([P, 2, ROW_TILES]), in1=shifts[:])
+        nc.scalar.activation(out=weights[:], in_=gaps[:], func=ACT.Exp)
         nc.scalar.activation(out=log_pos[:], in_=sums[:, POS, :], func=ACT.Ln)
         nc.vector.tensor_mul(out=weighted[:], in0=sums[:], in1=weights[:])
         nc.vector.tensor_add(out=total[:], in0=weighted[:, POS, :], in1=weighted[:, NEG, :])
         nc.scalar.activation(out=log_total[:], in_=total[:], func=ACT.Ln)
-        nc.vector.scalar_tensor_tensor(
-            out=numerator[:], in0=gaps[:, POS, :], scalar=1.0 / TEMPERATURE, in1=log_pos[:], op0=ALU.mult, op1=ALU.add
-        )
+        nc.vector.tensor_add(out=numerator[:], in0=gaps[:, POS, :], in1=log_pos[:])
         nc.vector.tensor_sub(out=result[:, :ROW_TILES], in0=numerator[:], in1=log_total[:])
         turned = turn_banks.tile([P, P], F32, tag="bank")
         nc.tensor.transpose(turned[:], result[:], identity[:])

from contextlib import ExitStack

import concourse.masks as masks
import concourse.mybir as mybir

F32 = mybir.dt.float32
BF16 = mybir.dt.bfloat16
U32 = mybir.dt.uint32
U8 = mybir.dt.uint8
FP8X4 = mybir.dt.float8_e4m3fn_x4
ACT = mybir.ActivationFunctionType
ALU = mybir.AluOpType

P = 128
PACK = 4
K_PASS = P * PACK
ROWS = 512
ROW_TILES = ROWS // P
FEATURES = 8192
PASSES = FEATURES // K_PASS
LOAD_PASSES = 2
LOAD_FEATURES = LOAD_PASSES * K_PASS
LOADS = PASSES // LOAD_PASSES
ALL_LOADS = 2 * LOADS
LOADS_AHEAD = 6
BANK_TILES = 2
UPPER_TILES = (0, 1)
LOWER_TILES = (2, 3)
HALF = ROWS // 2
TEMPERATURE = 0.07
MASKED = -1.0e30
POS, NEG = 0, 1

FLOPS = 2 * 2 * ROWS * ROWS * FEATURES


def tile_crossgenderinfonceloss_pa_k_kernel(tc, anchor, pos, out):
    nc = tc.nc
    with ExitStack() as ctx:
        const = ctx.enter_context(tc.tile_pool(name="const", bufs=1))
        keep = ctx.enter_context(tc.tile_pool(name="keep", bufs=1))
        raw_pool = ctx.enter_context(tc.tile_pool(name="raw", bufs=LOADS_AHEAD + 1))
        grouped_pool = ctx.enter_context(tc.tile_pool(name="grouped", bufs=3))
        sum_banks = ctx.enter_context(tc.psum_pool(name="sum_banks", bufs=1))
        turn_banks = ctx.enter_context(tc.psum_pool(name="turn_banks", bufs=4))
        ctx.enter_context(tc.manual_schedule())

        sources = [x.rearrange("(i p) k -> p i k", p=P) for x in (anchor, pos)]

        codes = keep.tile([P, 2 * PASSES * ROWS], U32, align_bytes=64)
        scales = keep.tile([P, 2 * PASSES * ROWS], U8, align_bytes=64)

        neg_logits = keep.tile([P, ROW_TILES, ROWS], F32)
        negated = keep.tile([P, 2, ROW_TILES, ROWS], F32)
        shifts = keep.tile([P, 2, ROW_TILES], F32)
        sums = keep.tile([P, 2, ROW_TILES], F32)

        def start_load(n):
            raw = raw_pool.tile([P, ROW_TILES, LOAD_FEATURES], BF16)
            feature = (n % LOADS) * LOAD_FEATURES
            nc.sync.dma_start(out=raw[:], in_=sources[n // LOADS][:, :, feature : feature + LOAD_FEATURES])
            return raw

        def transpose_load(raw):
            grouped = grouped_pool.tile([P, LOAD_PASSES, ROWS, PACK], BF16, align_bytes=64)
            raw_words = raw[:].bitcast(F32)
            grouped_words = grouped[:].bitcast(F32)
            for g in range(LOAD_PASSES):
                for b in range(ROW_TILES // BANK_TILES):
                    bank = turn_banks.tile([P, 2, BANK_TILES * P], F32)
                    for j in range(BANK_TILES):
                        for u in range(2):
                            word = (2 * g + u) * P
                            nc.tensor.transpose(
                                bank[:, u, j * P : (j + 1) * P],
                                raw_words[:, b * BANK_TILES + j, word : word + P],
                                identity[:],
                            )
                    copy_out = nc.scalar.copy if b % 2 == 0 else nc.vector.tensor_copy
                    columns = slice(b * BANK_TILES * P, (b + 1) * BANK_TILES * P)
                    copy_out(out=grouped_words[:, g, columns, :], in_=bank[:].rearrange("q u r -> q r u"))
            return grouped

        def quantise_load(n, grouped):
            columns = slice(n * LOAD_PASSES * ROWS, (n + 1) * LOAD_PASSES * ROWS)
            nc.vector.quantize_mx(
                out=codes[:, columns].bitcast(FP8X4),
                scales=scales[:, columns],
                in_=grouped[:].rearrange("q g r t -> q (g r t)"),
            )

        def new_sums():
            return [sum_banks.tile([P, ROWS], F32, name="sum%d" % i, tag="sum%d" % i) for i in range(ROW_TILES)]

        def multiply_load(n, banks):
            for i in range(ROW_TILES):
                left_out = HALF if n < LOADS and i in LOWER_TILES else 0
                for g in range(LOAD_PASSES):
                    c = (n % LOADS) * LOAD_PASSES + g
                    stationary = slice(c * ROWS + i * P, c * ROWS + (i + 1) * P)
                    moving = slice((n * LOAD_PASSES + g) * ROWS + left_out, (n * LOAD_PASSES + g + 1) * ROWS)
                    nc.tensor.matmul_mx(
                        out=banks[i][:, left_out:],
                        lhsT=codes[:, stationary].bitcast(FP8X4),
                        lhsT_scale=scales[:, stationary],
                        rhs=codes[:, moving].bitcast(FP8X4),
                        rhs_scale=scales[:, moving],
                        start=(c == 0),
                        stop=(c == PASSES - 1),
                    )

        def sim_neg_leaves_psum(tiles, banks):
            for i in tiles:
                copy_out = nc.scalar.copy if i % 2 == 0 else nc.vector.tensor_copy
                copy_out(out=neg_logits[:, i, :], in_=banks[i][:])

        def mirror_sim_neg(banks):
            for i in LOWER_TILES:
                for j in UPPER_TILES:
                    nc.tensor.transpose(banks[i][:, j * P : (j + 1) * P], neg_logits[:, j, i * P : (i + 1) * P], identity[:])

        def sum_exponentials(which, i, logits):
            one = slice(i, i + 1)
            nc.vector.tensor_scalar(
                out=negated[:, which, i, :],
                in0=logits,
                scalar1=-1.0 / TEMPERATURE,
                scalar2=None,
                op0=ALU.mult,
                op1=ALU.min,
                accum_out=shifts[:, which, one],
            )
            nc.scalar.activation(
                out=negated[:, which, i, :],
                in_=negated[:, which, i, :],
                func=ACT.Exp,
                bias=shifts[:, which, one],
                scale=-1.0,
                accum_out=sums[:, which, one],
            )

        raws = {}
        for n in range(LOADS_AHEAD):
            raws[n] = start_load(n)

        identity = const.tile([P, P], F32)
        masks.make_identity(nc, identity[:])
        masked_diagonal = const.tile([P, P], F32)
        nc.vector.tensor_scalar_mul(out=masked_diagonal[:], in0=identity[:], scalar1=MASKED)
        result = keep.tile([P, P], F32)
        nc.vector.memset(result[:], 0.0)
        warm = const.tile([P, 1], F32)
        nc.vector.memset(warm[:], 0.0)
        nc.scalar.activation(out=warm[:], in_=warm[:], func=ACT.Exp)

        banks = new_sums()
        for n in range(ALL_LOADS):
            if n + LOADS_AHEAD < ALL_LOADS:
                raws[n + LOADS_AHEAD] = start_load(n + LOADS_AHEAD)
            grouped = transpose_load(raws[n])
            if n == LOADS + 1:
                mirror_sim_neg(banks)
                sim_neg_leaves_psum(LOWER_TILES, banks)
                banks = new_sums()
            if n > 0:
                multiply_load(n - 1, banks)
            quantise_load(n, grouped)
            if n == LOADS:
                sim_neg_leaves_psum(UPPER_TILES, banks)
            i = n - (LOADS + 2)
            if 0 <= i < ROW_TILES:
                diagonal = neg_logits[:, i, i * P : (i + 1) * P]
                nc.vector.tensor_add(out=diagonal, in0=diagonal, in1=masked_diagonal[:])
                sum_exponentials(NEG, i, neg_logits[:, i, :])
        multiply_load(ALL_LOADS - 1, banks)
        for i in range(ROW_TILES):
            sum_exponentials(POS, i, banks[i][:])

        minus_top = keep.tile([P, ROW_TILES], F32)
        gaps = keep.tile([P, 2, ROW_TILES], F32)
        weights = keep.tile([P, 2, ROW_TILES], F32)
        weighted = keep.tile([P, 2, ROW_TILES], F32)
        total = keep.tile([P, ROW_TILES], F32)
        log_pos = keep.tile([P, ROW_TILES], F32)
        log_total = keep.tile([P, ROW_TILES], F32)
        numerator = keep.tile([P, ROW_TILES], F32)
        nc.vector.tensor_tensor(out=minus_top[:], in0=shifts[:, POS, :], in1=shifts[:, NEG, :], op=ALU.min)
        nc.vector.tensor_sub(out=gaps[:], in0=minus_top[:].unsqueeze(1).to_broadcast([P, 2, ROW_TILES]), in1=shifts[:])
        nc.scalar.activation(out=weights[:], in_=gaps[:], func=ACT.Exp)
        nc.scalar.activation(out=log_pos[:], in_=sums[:, POS, :], func=ACT.Ln)
        nc.vector.tensor_mul(out=weighted[:], in0=sums[:], in1=weights[:])
        nc.vector.tensor_add(out=total[:], in0=weighted[:, POS, :], in1=weighted[:, NEG, :])
        nc.scalar.activation(out=log_total[:], in_=total[:], func=ACT.Ln)
        nc.vector.tensor_add(out=numerator[:], in0=gaps[:, POS, :], in1=log_pos[:])
        nc.vector.tensor_sub(out=result[:, :ROW_TILES], in0=numerator[:], in1=log_total[:])
        turned = turn_banks.tile([P, P], F32, tag="bank")
        nc.tensor.transpose(turned[:], result[:], identity[:])
        result_rows = keep.tile([P, P], F32)
        nc.vector.tensor_copy(out=result_rows[:], in_=turned[:])
        nc.sync.dma_start(out=out.rearrange("(i p) -> i p", p=P), in_=result_rows[:ROW_TILES, :])
